import numpy as np
import ml_dtypes


def mxq(x, axis, fmt="e4m3"):
    dtype, down = {"e4m3": (ml_dtypes.float8_e4m3fn, 7), "e5m2": (ml_dtypes.float8_e5m2, 14)}[fmt]
    v = np.moveaxis(np.asarray(x, np.float32).astype(ml_dtypes.bfloat16).astype(np.float64), axis, -1)
    blocks = v.reshape(v.shape[:-1] + (-1, 32))
    amax = np.abs(blocks).max(-1, keepdims=True)
    byte = np.maximum(np.where(amax > 0, np.frexp(amax)[1] - 1 + 127, 0) - down, 1)
    scale = np.exp2(byte - 127.0)
    codes = (blocks / scale).astype(np.float32).astype(dtype).astype(np.float64)
    return np.moveaxis((codes * scale).reshape(v.shape), -1, axis)


WIDE = False


def mx_kscale(k):
    if not WIDE:
        return np.ones(k)
    levels = np.array([18, -18])
    if k % 512:
        return np.exp2(np.random.permutation(np.resize(levels, k // 32))).repeat(32)
    a = np.empty((k // 512, 16))
    for p in range(k // 512):
        a[p, :8] = np.random.permutation(np.resize(levels, 8))
        for g in range(8):
            far = levels[np.abs(levels - a[p, g]) >= 10]
            a[p, g + 8] = far[np.random.randint(len(far))]
    return np.exp2(a.ravel()).repeat(32)


BF16 = ml_dtypes.bfloat16


def bf(x):
    return np.asarray(x, np.float32).astype(BF16)


def f64(x):
    return np.asarray(x).astype(np.float64)


B, C, L = 32, 16, 4096
LEVEL = 3
NODES = 2 ** LEVEL
D = L // NODES
T = B * C * NODES
INV_SQRT2 = 0.7071067811865476


def haar_wpt(x, level):
    c = x[:, :, None, :]
    for _ in range(level):
        Bn, Cn, N, n = c.shape
        y = c.reshape(Bn, Cn, N, n // 2, 2)
        a = (y[..., 0] + y[..., 1]) * INV_SQRT2
        d = (y[..., 0] - y[..., 1]) * INV_SQRT2
        c = np.stack([a, d], axis=3).reshape(Bn, Cn, N * 2, n // 2)
    return c


def haar_iwpt(c, level):
    for _ in range(level):
        a = c[:, :, 0::2, :]
        d = c[:, :, 1::2, :]
        even = (a + d) * INV_SQRT2
        odd = (a - d) * INV_SQRT2
        Bn, Cn, N2, n = even.shape
        c = np.stack([even, odd], axis=-1).reshape(Bn, Cn, N2, 2 * n)
    return c[:, :, 0, :]


def gate_values(x, W, b, threshold):
    coeffs = haar_wpt(f64(x), LEVEL)
    z = coeffs @ f64(W).T + f64(b)
    raw = coeffs / (1.0 + np.exp(-z))
    return z, raw, np.where(np.abs(raw) < f64(threshold), 0.0, raw)


def setup_inputs():
    x0 = bf(np.random.standard_normal((B * C, 1, L)))
    W0 = bf(np.random.standard_normal((D, D)) / np.sqrt(D))
    b = bf(np.random.standard_normal(D) * 0.1)
    threshold = bf(np.random.uniform(0.08, 0.12, 1))
    rows = np.arange(B * C)
    while rows.size > 0:
        raw = gate_values(x0[rows], W0, b, threshold)[1]
        near = np.abs(np.abs(raw) - f64(threshold)).min(axis=(1, 2, 3)) < 1e-4
        rows = rows[near]
        x0[rows] = bf(np.random.standard_normal((rows.size, 1, L)))
    x0 = x0.reshape(B, C, L)
    z, _, gated = gate_values(x0, W0, b, threshold)
    s = mx_kscale(T)[::NODES].reshape(B, C, 1)
    u = mx_kscale(D)
    u = u / u.max()
    g = np.random.standard_normal((B, C, L)) * np.exp2(np.random.randint(-6, 1, (B, C, 1)))
    return {"x": bf(f64(x0) * s),
            "W": bf(f64(W0) / u[:, None]),
            "b": b,
            "threshold": threshold,
            "z": np.asarray(z, np.float32),
            "gated": np.asarray(gated, np.float32),
            "grad_out": bf(g / s * np.repeat(u, NODES))}


def reference(x, W, b, threshold, z, gated, grad_out):
    g = f64(grad_out)
    h = f64(gated)
    gate = 1.0 / (1.0 + np.exp(-f64(z)))
    dh = haar_wpt(g, LEVEL)
    dz = (dh * h * (1.0 - gate)).reshape(T, D)
    coeffs = haar_wpt(f64(x), LEVEL).reshape(T, D)
    dm = mxq(dz, 1, "e5m2") @ mxq(f64(W), 0, "e4m3")
    dW = mxq(dz, 0, "e5m2").T @ mxq(coeffs, 0, "e4m3")
    dcoeffs = dm.reshape(B, C, NODES, D) + np.where(h != 0.0, dh * gate, 0.0)
    dx = haar_iwpt(dcoeffs, LEVEL) + g
    return dx, dW

@@ -1,0 +1,500 @@
+from contextlib import ExitStack
+import math
+
+import concourse.mybir as mybir
+from concourse.masks import make_identity
+
+ROWS = 512
+L = 4096
+NODES = 8
+D = 512
+P = 128
+
+FLOPS = 2 * (2 * ROWS * NODES * D * D)
+BYTES = 2 * ROWS * L * 2 + D * D * 2 + 2 * ROWS * L * 4 + ROWS * L * 4 + D * D * 4
+
+F32 = mybir.dt.float32
+BF16 = mybir.dt.bfloat16
+I32 = mybir.dt.int32
+U32 = mybir.dt.uint32
+U8 = mybir.dt.uint8
+E4 = mybir.dt.float8_e4m3fn_x4
+E5 = mybir.dt.float8_e5m2_x4
+OP = mybir.AluOpType
+ACT = mybir.ActivationFunctionType
+
+C = 1.0 / math.sqrt(8.0)
+SQ8 = math.sqrt(8.0)
+
+E_PE = 384
+E_DVE = D - E_PE
+NB = E_PE // 64
+
+
+def tile_waveletgatednet_v_kernel(tc, x, W, b, threshold, z, gated, grad_out, out_0, out_1):
+    nc = tc.nc
+    V, S, T, G, SY = nc.vector, nc.scalar, nc.tensor, nc.gpsimd, nc.sync
+
+    x2 = x.rearrange("b c l -> (b c) l")
+    g2 = grad_out.rearrange("b c l -> (b c) l")
+    o2 = out_0.rearrange("b c l -> (b c) l")
+    z2 = z.rearrange("b c n e -> (b c) n e")
+    h2 = gated.rearrange("b c n e -> (b c) n e")
+
+    with ExitStack() as ctx:
+        const = ctx.enter_context(tc.tile_pool(name="const", bufs=1))
+        one = ctx.enter_context(tc.tile_pool(name="one", bufs=1))
+        two = ctx.enter_context(tc.tile_pool(name="two", bufs=2))
+        lev = ctx.enter_context(tc.tile_pool(name="lev", bufs=2))
+        keep = ctx.enter_context(tc.tile_pool(name="keep", bufs=1))
+        ps = ctx.enter_context(tc.psum_pool(name="ps", bufs=2))
+
+        ident_f = const.tile([P, P], F32, name="ident_f")
+        make_identity(nc, ident_f[:])
+        ident_b = const.tile([P, P], BF16, name="ident_b")
+        make_identity(nc, ident_b[:])
+        pidx = const.tile([P, 1], I32, name="pidx")
+        G.iota(pidx[:], [[0, 1]], base=0, channel_multiplier=1)
+        podd = const.tile([P, 1], I32, name="podd")
+        V.tensor_single_scalar(podd[:], pidx[:], 1, OP.bitwise_and)
+        poddf = const.tile([P, 1], F32, name="poddf")
+        V.tensor_copy(poddf[:], podd[:])
+        sgn = const.tile([P, 1], F32, name="sgn")
+        V.tensor_scalar(sgn[:], poddf[:], -2.0, 1.0, OP.mult, OP.add)
+
+        def wpt(src, y1, y2, dst, E):
+            s = src.rearrange("p (a two) -> p a two", two=2)
+            for i, op in ((0, OP.add), (1, OP.subtract)):
+                V.tensor_tensor(y1[:, i * 4 * E:(i + 1) * 4 * E], s[:, :, 0], s[:, :, 1], op)
+            s = y1.rearrange("p (a two) -> p a two", two=2)
+            o = y2.rearrange("p (b c f) -> p b c f", b=2, c=2)
+            s4 = y1.rearrange("p (b a two) -> p b a two", b=2, two=2)
+            for i, op in ((0, OP.add), (1, OP.subtract)):
+                V.tensor_tensor(o[:, :, i, :], s4[:, :, :, 0], s4[:, :, :, 1], op)
+            s4 = y2.rearrange("p (b a two) -> p b a two", b=4, two=2)
+            o = dst.rearrange("p (b c) e -> p b c e", c=2)
+            for i, op in ((0, OP.add), (1, OP.subtract)):
+                V.tensor_tensor(o[:, :, i, :], s4[:, :, :, 0], s4[:, :, :, 1], op)
+
+        Hm = const.tile([P, NODES, 16], BF16, name="Hm")
+        h1 = const.tile([P, P], BF16, name="h1")
+        hh2 = const.tile([P, P], BF16, name="hh2")
+        wpt(ident_b[:], h1[:], hh2[:], Hm[:], 16)
+
+        wc = const.tile([P, D], U32, name="wc", align_bytes=64)
+        ws = const.tile([P, D], U8, name="ws", align_bytes=64)
+
+        wr = {}
+
+        def load_w():
+            wr[0] = two.tile([P, 4, D], BF16, name="wraw", tag="ap")
+            SY.dma_start(out=wr[0][:], in_=W.rearrange("(p j) d -> p j d", j=4))
+
+        def do_w():
+            wg = one.tile([P, D, 4], BF16, name="wg", tag="ai", align_bytes=64)
+            S.copy(out=wg[:], in_=wr[0][:].rearrange("p j d -> p d j"))
+            V.quantize_mx(out=wc[:].bitcast(E4), scales=ws[:], in_=wg[:].rearrange("p d j -> p (d j)"))
+
+        xc = [keep.tile([P, D], U32, name="xc%d" % g, align_bytes=64) for g in range(8)]
+        xs = [keep.tile([P, D], U8, name="xs%d" % g, align_bytes=64) for g in range(8)]
+        dc = [keep.tile([P, D], U32, name="dc%d" % g, align_bytes=64) for g in range(8)]
+        ds = [keep.tile([P, D], U8, name="ds%d" % g, align_bytes=64) for g in range(8)]
+        xr = {}
+        pending = []
+
+        def load_x(g):
+            if g == 1:
+                whole = one.tile([P, 2, 2048], BF16, name="xr1", tag="ny")
+            for hf in range(2):
+                t = whole[:, hf, :] if g == 1 else two.tile([P, 2048], BF16, name="xr", tag="xr", bufs=2)[:, :]
+                for h in range(2):
+                    SY.dma_start(out=t[h::2, :], in_=x2[64 * g:64 * g + 64, 2048 * hf:2048 * hf + 2048])
+                xr[g, hf] = t
+
+        def do_x(g):
+            E = 256
+            xi = two.tile([P, D, 4], BF16, name="xi", tag="xi", align_bytes=64)
+            a1, a2 = [], []
+
+            def l1():
+                for hf in range(2):
+                    t = xr[g, hf].rearrange("p (a two) -> p a two", two=2)
+                    y1 = lev.tile([P, 1024], F32, name="lA", tag="lA", bufs=3)
+                    V.scalar_tensor_tensor(out=y1[:], in0=t[:, :, 1], scalar=sgn[:], in1=t[:, :, 0], op0=OP.mult, op1=OP.add)
+                    a1.append(y1)
+
+            def l2():
+                for hf in range(2):
+                    y2 = lev.tile([P, 1024], F32, name="lB", tag="lB", bufs=2)
+                    s = a1[hf][:].rearrange("p (a two) -> p a two", two=2)
+                    for i, op in ((0, OP.add), (1, OP.subtract)):
+                        V.tensor_tensor(y2[:, 512 * i:512 * i + 512], s[:, :, 0], s[:, :, 1], op)
+                    a2.append(y2)
+
+            def l3():
+                for hf in range(2):
+                    y3 = lev.tile([P, 4, E], F32, name="lA", tag="lA", bufs=3)
+                    s = a2[hf][:].rearrange("p (b a two) -> p b a two", b=2, two=2)
+                    o = y3[:].rearrange("p (b c) e -> p b c e", c=2)
+                    for i, op in ((0, OP.add), (1, OP.subtract)):
+                        V.tensor_tensor(o[:, :, i, :], s[:, :, :, 0], s[:, :, :, 1], op)
+                    S.activation(out=xi[:, E * hf:E * hf + E, :], in_=y3[:].rearrange("p t e -> p e t"), func=ACT.Copy, scale=C)
+                pending.append(lambda: V.quantize_mx(out=xc[g][:].bitcast(E4), scales=xs[g][:], in_=xi[:].rearrange("p e t -> p (e t)")))
+
+            return [l1, l2, l3]
+
+        def flush():
+            while pending:
+                pending[0]()
+                pending.remove(pending[0])
+
+        def wpt_parts(src, E):
+            t = {}
+
+            def l1():
+                t[1] = lev.tile([P, 8 * E], F32, name="lA", tag="lA", bufs=3)
+                s = src.rearrange("p (a two) -> p a two", two=2)
+                for i, op in ((0, OP.add), (1, OP.subtract)):
+                    V.tensor_tensor(t[1][:, i * 4 * E:(i + 1) * 4 * E], s[:, :, 0], s[:, :, 1], op)
+
+            def l2():
+                t[2] = lev.tile([P, 8 * E], F32, name="lB", tag="lB", bufs=2)
+                s = t[1][:].rearrange("p (b a two) -> p b a two", b=2, two=2)
+                o = t[2][:].rearrange("p (b c f) -> p b c f", b=2, c=2)
+                for i, op in ((0, OP.add), (1, OP.subtract)):
+                    V.tensor_tensor(o[:, :, i, :], s[:, :, :, 0], s[:, :, :, 1], op)
+
+            def l3():
+                t[3] = lev.tile([P, NODES, E], F32, name="lA", tag="lA", bufs=3)
+                s = t[2][:].rearrange("p (b a two) -> p b a two", b=4, two=2)
+                o = t[3][:].rearrange("p (b c) e -> p b c e", c=2)
+                for i, op in ((0, OP.add), (1, OP.subtract)):
+                    V.tensor_tensor(o[:, :, i, :], s[:, :, :, 0], s[:, :, :, 1], op)
+
+            return [l1, l2, l3, lambda: t[3]]
+
+        zt, ht, gt, dz, dct, dst_, ny = {}, {}, {}, {}, {}, {}, {}
+
+        def load_z(i):
+            zt[i] = two.tile([P, NODES, D], F32, name="zt", tag="zt", bufs=3)
+            for hf in range(2):
+                n = slice(4 * hf, 4 * hf + 4)
+                SY.dma_start(out=zt[i][:, n, :], in_=z2[P * i:P * i + P, n, :])
+
+        def load_h(i):
+            ht[i] = two.tile([P, NODES, D], F32, name="ht", tag="ht")
+            for hf in range(2):
+                n = slice(4 * hf, 4 * hf + 4)
+                SY.dma_start(out=ht[i][:, n, :], in_=h2[P * i:P * i + P, n, :])
+
+        def load_g(i):
+            gt[i] = one.tile([P, L], BF16, name="gt", tag="gt")
+            SY.dma_start(out=gt[i][:], in_=g2[P * i:P * i + P, :])
+
+        def kq(i):
+            def k(hf):
+                n = slice(4 * hf, 4 * hf + 4)
+                V.scalar_tensor_tensor(out=zt[i][:, n, :], in0=ht[i][:, n, :], scalar=0.0, in1=zt[i][:, n, :], op0=OP.not_equal, op1=OP.mult)
+
+            def q(hf):
+                n = slice(4 * hf, 4 * hf + 4)
+                V.scalar_tensor_tensor(out=ht[i][:, n, :], in0=zt[i][:, n, :], scalar=1.0, in1=ht[i][:, n, :], op0=OP.subtract, op1=OP.mult)
+
+            return [lambda: k(0), lambda: k(1), lambda: q(0), lambda: q(1)]
+
+        def gate_half(i, hf):
+            n = slice(4 * hf, 4 * hf + 4)
+            S.activation(out=zt[i][:, n, :], in_=zt[i][:, n, :], func=ACT.Sigmoid)
+
+        def products(i):
+            k, q = zt[i], ht[i]
+
+            def pair(e0, w, dh):
+                sl = slice(e0, e0 + w)
+                V.scalar_tensor_tensor(out=dz[i][:, :, sl], in0=dh, scalar=-C, in1=q[:, :, sl], op0=OP.mult, op1=OP.mult)
+                V.scalar_tensor_tensor(out=k[:, :, sl], in0=k[:, :, sl], scalar=1.0, in1=dh, op0=OP.add, op1=OP.mult)
+
+            gTs, dhs = {}, {}
+
+            def prep(bk):
+                tp = ps.tile([P, 4, P], BF16, name="tp", tag="tp")
+                for c in range(4):
+                    p0 = (4 * bk + c) * P
+                    T.transpose(tp[:, c, :], gt[i][:, p0:p0 + P], ident_b[:])
+                gTs[bk] = two.tile([P, 4, P], BF16, name="gT", tag="gT", bufs=4)
+                S.copy(out=gTs[bk][:], in_=tp[:])
+
+            def mm(bk):
+                dhs[bk] = ps.tile([P, NODES, 64], F32, name="dh", tag="dh")
+                for c in range(4):
+                    T.matmul(dhs[bk][:, :, 16 * c:16 * c + 16], lhsT=gTs[bk][:, c, :], rhs=Hm[:], start=True, stop=True)
+
+            lv = wpt_parts(gt[i][:, 8 * E_PE:], E_DVE)
+
+            def early():
+                dz[i] = one.tile([P, NODES, D], BF16, name="dz", tag="dz")
+                prep(0)
+                prep(1)
+                prep(2)
+                mm(0)
+                mm(1)
+
+            def bank(bk):
+                pair(64 * bk, 64, dhs[bk][:])
+                if bk < 3:
+                    lv[bk]()
+                if bk == 4:
+                    pair(E_PE, E_DVE, lv[3]()[:])
+
+            def ahead(bk):
+                if bk + 2 < NB:
+                    mm(bk + 2)
+                if bk + 3 < NB:
+                    prep(bk + 3)
+
+            return early, bank, ahead
+
+        def features(i):
+            w = dz[i][:].rearrange("p n e -> p (n e)").bitcast(F32)
+            tis = []
+            for hf in range(2):
+                ti = two.tile([P, 4, P, 4], BF16, name="ti", tag="ti", align_bytes=64)
+                for pr in range(2):
+                    rt = ps.tile([P, 2, 2, P], F32, name="tp", tag="tp")
+                    for m in range(2):
+                        n = 4 * hf + 2 * pr + m
+                        for u in range(2):
+                            T.transpose(rt[:, m, u, :], w[:, 256 * n + u:256 * n + 256:2], ident_f[:])
+                    o = ti[:, 2 * pr:2 * pr + 2, :, :].rearrange("p m r t -> p (m r t)").bitcast(F32)
+                    S.copy(out=o.rearrange("p (m r u) -> p m r u", m=2, u=2), in_=rt[:].rearrange("p m u r -> p m r u"))
+                tis.append(ti)
+
+            return tis
+
+        def quant_features(i, tis):
+            dct[i], dst_[i] = [], []
+
+            def half(ti):
+                c = two.tile([P, D], U32, name="dct", tag="dct", bufs=2, align_bytes=64)
+                s = two.tile([P, D], U8, name="dst", tag="dst", bufs=2, align_bytes=64)
+                V.quantize_mx(out=c[:].bitcast(E5), scales=s[:], in_=ti[:].rearrange("p n r t -> p (n r t)"))
+                dct[i].append(c)
+                dst_[i].append(s)
+
+            return [lambda ti=ti: half(ti) for ti in tis]
+
+        aps = {}
+
+        def move(i):
+            for hf in range(2):
+                aps[hf] = two.tile([P, 4, D], BF16, name="ap", tag="ap")
+                for h in range(2):
+                    SY.dma_start(out=aps[hf][h::2, :, :], in_=dz[i][64 * hf:64 * hf + 64, 4 * h:4 * h + 4, :])
+
+        def tokens(i, hf):
+            ai = one.tile([P, D, 4], BF16, name="ai", tag="ai", align_bytes=64)
+            S.copy(out=ai[:], in_=aps[hf][:].rearrange("p t e -> p e t"))
+            g = 2 * i + hf
+            pending.append(lambda: V.quantize_mx(out=dc[g][:].bitcast(E5), scales=ds[g][:], in_=ai[:].rearrange("p e t -> p (e t)")))
+
+        def back(i):
+            y = zt[i]
+            ny[i] = one.tile([P, 6, D], F32, name="ny", tag="ny")
+
+            dms = {}
+
+            def mul(n):
+                m = n % 4
+                dms[n] = ps.tile([P, D], F32, name="mm", tag="mm")
+                T.matmul_mx(out=dms[n][:], lhsT=dct[i][n // 4][:, P * m:P * m + P].bitcast(E5), lhsT_scale=dst_[i][n // 4][:, P * m:P * m + P],
+                            rhs=wc[:].bitcast(E4), rhs_scale=ws[:], start=True, stop=True)
+
+            def add(n):
+                V.scalar_tensor_tensor(out=y[:, n, :], in0=dms[n][:], scalar=SQ8, in1=y[:, n, :], op0=OP.mult, op1=OP.add)
+                if n >= 2:
+                    G.tensor_scalar(ny[i][:, n - 2, :], y[:, n, :], -1.0, 0.0, OP.mult, OP.add)
+
+            return mul, add
+
+        def hops(i, dve=()):
+            ts, tns, obs = {}, {}, {}
+
+            def first(db, b3):
+                if b3 == 0:
+                    ts[db] = two.tile([P, 2, 4, P], F32, name="t", tag="t")
+                    tns[db] = two.tile([P, 4, P], F32, name="tn", tag="tn")
+                hop = ps.tile([P, 4, P], F32, name="hop", tag="hop")
+                for o in range(4):
+                    j1, j0 = o // 2, o % 2
+                    for q in range(4):
+                        b1, b2 = q // 2, q % 2
+                        n = 4 * b1 + 2 * b2 + b3
+                        sl = slice(P * db, P * db + P)
+                        src = ny[i][:, n - 2, sl] if (b1 * j0 + b2 * j1) % 2 else zt[i][:, n, sl]
+                        T.matmul(hop[:, o, :], lhsT=src, rhs=ident_f[:], start=(q == 0), stop=(q == 3), is_transpose=True)
+                if (0, db, b3) in dve:
+                    V.tensor_copy(out=ts[db][:, b3, :, :], in_=hop[:])
+                else:
+                    S.copy(out=ts[db][:, b3, :, :], in_=hop[:])
+                if b3 == 1:
+                    S.mul(tns[db][:], hop[:], -1.0)
+
+            def second(db, j2):
+                if j2 == 0:
+                    obs[db] = two.tile([P, P, NODES], F32, name="ob", tag="ob")
+                hop = ps.tile([P, 4, P], F32, name="hop", tag="hop")
+                for o in range(4):
+                    T.matmul(hop[:, o, :], lhsT=ts[db][:, 0, o, :], rhs=ident_f[:], start=True, stop=False, is_transpose=True)
+                    s = tns[db][:, o, :] if j2 else ts[db][:, 1, o, :]
+                    T.matmul(hop[:, o, :], lhsT=s, rhs=ident_f[:], start=False, stop=True, is_transpose=True)
+                if (1, db, j2) in dve:
+                    V.tensor_scalar_mul(obs[db][:, :, 4 * j2:4 * j2 + 4], hop[:].rearrange("p o d -> p d o"), 0.125)
+                else:
+                    S.activation(out=obs[db][:, :, 4 * j2:4 * j2 + 4], in_=hop[:].rearrange("p o d -> p d o"), func=ACT.Copy, scale=0.125)
+                if j2 == 1:
+                    SY.dma_start(out=o2[P * i:P * i + P, 1024 * db:1024 * db + 1024], in_=obs[db][:].rearrange("p d j -> p (d j)"))
+
+            out = []
+            for db in range(5):
+                for s in range(2):
+                    if db < 4:
+                        out.append(lambda db=db, s=s: first(db, s))
+                    if db > 0:
+                        out.append(lambda db=db, s=s: second(db - 1, s))
+            return out
+
+        accs = {}
+
+        def weight_gradient(gs):
+            for g in gs:
+                for mt in range(4):
+                    if g == 0:
+                        accs[mt] = ps.tile([P, D], F32, name="acc", tag="dh" if mt < 2 else "tp")
+                    msl = slice(P * mt, P * mt + P)
+                    T.matmul_mx(out=accs[mt][:], lhsT=dc[g][:, msl].bitcast(E5), lhsT_scale=ds[g][:, msl],
+                                rhs=xc[g][:].bitcast(E4), rhs_scale=xs[g][:], start=(g == 0), stop=(g == 7))
+
+        def store_weight_gradient():
+            for mt in range(4):
+                r1 = lev.tile([P, D], F32, name="r1", tag="lA" if mt < 2 else "lB", bufs=3 if mt < 2 else 2)
+                if mt % 2:
+                    S.copy(out=r1[:], in_=accs[mt][:])
+                else:
+                    V.tensor_copy(out=r1[:], in_=accs[mt][:])
+                SY.dma_start(out=out_1[P * mt:P * mt + P, :], in_=r1[:])
+
+        def weave(first, second):
+            n = max(len(first), 1)
+            for j in range(n):
+                if j < len(first):
+                    first[j]()
+                for s in second[len(second) * j // n:len(second) * (j + 1) // n]:
+                    s()
+
+        def run(ps):
+            for p in ps:
+                p()
+
+        N_HOP_X = 5
+        N_HOP_P = 7
+        LAST = {(0, 3, 0), (0, 3, 1), (1, 2, 1), (1, 3, 0)}
+
+        with tc.manual_schedule():
+            load_x(0)
+            load_x(1)
+            load_z(0)
+            load_h(0)
+            load_g(0)
+            load_w()
+            load_z(1)
+            load_h(1)
+            run(do_x(0))
+            gate_half(0, 0)
+            gate_half(0, 1)
+            run(do_x(1))
+            early, bank, ahead = products(0)
+            early()
+            kq0 = kq(0)
+            run(kq0[:2])
+            flush()
+            run(kq0[2:])
+            do_w()
+            load_x(2)
+            gate_half(1, 0)
+            gate_half(1, 1)
+            for bk in range(NB):
+                bank(bk)
+                ahead(bk)
+            hop = []
+            for i in range(4):
+                if i < 3:
+                    load_g(i + 1)
+                move(i)
+                if i < 2:
+                    load_z(i + 2)
+                    load_h(i + 2)
+                f = features(i)
+                qf = quant_features(i, f)
+                if i < 3:
+                    early, bank, ahead = products(i + 1)
+                    kn = kq(i + 1)
+                else:
+                    kn = do_x(5)
+                run(kn[:2])
+                run(hop[:len(hop) // 2])
+                tokens(i, 0)
+                if i < 3:
+                    early()
+                run(hop[len(hop) // 2:])
+                if i == 3:
+                    weight_gradient(range(2))
+                qf[0]()
+                mul, add = back(i)
+                mul(0)
+                mul(1)
+                run(kn[2:])
+                qf[1]()
+                for n in range(NODES):
+                    add(n)
+                    if n + 2 < NODES:
+                        mul(n + 2)
+                if i < 2:
+                    gate_half(i + 2, 0)
+                    gate_half(i + 2, 1)
+                flush()
+                tokens(i, 1)
+                hop = hops(i, LAST if i == 3 else ())
+                if i < 3:
+                    weave(do_x(2 + i), hop[:N_HOP_X])
+                    load_x(3 + i)
+                    hop = hop[N_HOP_X:]
+                    for bk in range(NB):
+                        bank(bk)
+                        run(hop[N_HOP_P * bk // NB:N_HOP_P * (bk + 1) // NB])
+                        ahead(bk)
+                    hop = hop[N_HOP_P:]
+                    flush()
+            load_x(6)
+            load_x(7)
+            weight_gradient(range(2, 6))
+            xa, xb = do_x(6), do_x(7)
+            xa[0]()
+            run(hop[:1])
+            xa[1]()
+            run(hop[1:3])
+            xa[2]()
+            run(hop[3:4])
+            xb[0]()
+            run(hop[4:6])
+            flush()
+            xb[1]()
+            run(hop[6:8])
+            xb[2]()
+            run(hop[8:9])
+            weight_gradient([6])
+            run(hop[9:11])
+            flush()
+            run(hop[11:13])
+            weight_gradient([7])
+            store_weight_gradient()
+            run(hop[13:])

@@ -91,7 +91,7 @@ def tile_waveletgatednet_v_kernel(tc, x, W, b, threshold, z, gated, grad_out, ou
             SY.dma_start(out=wr[0][:], in_=W.rearrange("(p j) d -> p j d", j=4))
 
         def do_w():
-            wg = one.tile([P, D, 4], BF16, name="wg", tag="ai", align_bytes=64)
+            wg = two.tile([P, D, 4], BF16, name="wg", tag="ai", align_bytes=64)
             S.copy(out=wg[:], in_=wr[0][:].rearrange("p j d -> p d j"))
             V.quantize_mx(out=wc[:].bitcast(E4), scales=ws[:], in_=wg[:].rearrange("p d j -> p (d j)"))
 
@@ -103,10 +103,8 @@ def tile_waveletgatednet_v_kernel(tc, x, W, b, threshold, z, gated, grad_out, ou
         pending = []
 
         def load_x(g):
-            if g == 1:
-                whole = one.tile([P, 2, 2048], BF16, name="xr1", tag="ny")
             for hf in range(2):
-                t = whole[:, hf, :] if g == 1 else two.tile([P, 2048], BF16, name="xr", tag="xr", bufs=2)[:, :]
+                t = two.tile([P, 2048], BF16, name="xr", tag="xr", bufs=2)[:, :]
                 for h in range(2):
                     SY.dma_start(out=t[h::2, :], in_=x2[64 * g:64 * g + 64, 2048 * hf:2048 * hf + 2048])
                 xr[g, hf] = t
@@ -126,18 +124,19 @@ def tile_waveletgatednet_v_kernel(tc, x, W, b, threshold, z, gated, grad_out, ou
             def l2():
                 for hf in range(2):
                     y2 = lev.tile([P, 1024], F32, name="lB", tag="lB", bufs=2)
-                    s = a1[hf][:].rearrange("p (a two) -> p a two", two=2)
+                    s = a1[hf][:].rearrange("p (e f g) -> p e f g", f=2, g=2)
+                    o = y2[:].rearrange("p (f g e) -> p f e g", f=2, g=2)
                     for i, op in ((0, OP.add), (1, OP.subtract)):
-                        V.tensor_tensor(y2[:, 512 * i:512 * i + 512], s[:, :, 0], s[:, :, 1], op)
+                        V.tensor_tensor(o[:, i, :, :], s[:, :, 0, :], s[:, :, 1, :], op)
                     a2.append(y2)
 
             def l3():
                 for hf in range(2):
                     y3 = lev.tile([P, 4, E], F32, name="lA", tag="lA", bufs=3)
-                    s = a2[hf][:].rearrange("p (b a two) -> p b a two", b=2, two=2)
+                    s = a2[hf][:].rearrange("p (f g e) -> p f g e", f=2, g=2)
                     o = y3[:].rearrange("p (b c) e -> p b c e", c=2)
                     for i, op in ((0, OP.add), (1, OP.subtract)):
-                        V.tensor_tensor(o[:, :, i, :], s[:, :, :, 0], s[:, :, :, 1], op)
+                        V.tensor_tensor(o[:, i, :, :], s[:, :, 0, :], s[:, :, 1, :], op)
                     S.activation(out=xi[:, E * hf:E * hf + E, :], in_=y3[:].rearrange("p t e -> p e t"), func=ACT.Copy, scale=C)
                 pending.append(lambda: V.quantize_mx(out=xc[g][:].bitcast(E4), scales=xs[g][:], in_=xi[:].rearrange("p e t -> p (e t)")))
 
@@ -159,17 +158,18 @@ def tile_waveletgatednet_v_kernel(tc, x, W, b, threshold, z, gated, grad_out, ou
 
             def l2():
                 t[2] = lev.tile([P, 8 * E], F32, name="lB", tag="lB", bufs=2)
-                s = t[1][:].rearrange("p (b a two) -> p b a two", b=2, two=2)
-                o = t[2][:].rearrange("p (b c f) -> p b c f", b=2, c=2)
-                for i, op in ((0, OP.add), (1, OP.subtract)):
-                    V.tensor_tensor(o[:, :, i, :], s[:, :, :, 0], s[:, :, :, 1], op)
+                s = t[1][:].rearrange("p (b e f g) -> p b e f g", b=2, f=2, g=2)
+                o = t[2][:].rearrange("p (b f g e) -> p b f e g", b=2, f=2, g=2)
+                for b in range(2):
+                    for i, op in ((0, OP.add), (1, OP.subtract)):
+                        V.tensor_tensor(o[:, b, i, :, :], s[:, b, :, 0, :], s[:, b, :, 1, :], op)
 
             def l3():
                 t[3] = lev.tile([P, NODES, E], F32, name="lA", tag="lA", bufs=3)
-                s = t[2][:].rearrange("p (b a two) -> p b a two", b=4, two=2)
-                o = t[3][:].rearrange("p (b c) e -> p b c e", c=2)
+                o = t[3][:].rearrange("p (b c f) e -> p c b f e", b=2, c=2)
+                s2 = t[2][:].rearrange("p (b f g e) -> p g b f e", b=2, f=2, g=2)
                 for i, op in ((0, OP.add), (1, OP.subtract)):
-                    V.tensor_tensor(o[:, :, i, :], s[:, :, :, 0], s[:, :, :, 1], op)
+                    V.tensor_tensor(o[:, i, :, :, :], s2[:, 0, :, :, :], s2[:, 1, :, :, :], op)
 
             return [l1, l2, l3, lambda: t[3]]
 
@@ -236,6 +236,8 @@ def tile_waveletgatednet_v_kernel(tc, x, W, b, threshold, z, gated, grad_out, ou
                 prep(0)
                 prep(1)
                 prep(2)
+
+            def start():
                 mm(0)
                 mm(1)
 
@@ -252,7 +254,7 @@ def tile_waveletgatednet_v_kernel(tc, x, W, b, threshold, z, gated, grad_out, ou
                 if bk + 3 < NB:
                     prep(bk + 3)
 
-            return early, bank, ahead
+            return early, bank, ahead, start
 
         def features(i):
             w = dz[i][:].rearrange("p n e -> p (n e)").bitcast(F32)
@@ -292,75 +294,86 @@ def tile_waveletgatednet_v_kernel(tc, x, W, b, threshold, z, gated, grad_out, ou
                     SY.dma_start(out=aps[hf][h::2, :, :], in_=dz[i][64 * hf:64 * hf + 64, 4 * h:4 * h + 4, :])
 
         def tokens(i, hf):
-            ai = one.tile([P, D, 4], BF16, name="ai", tag="ai", align_bytes=64)
+            ai = two.tile([P, D, 4], BF16, name="ai", tag="ai", align_bytes=64)
             S.copy(out=ai[:], in_=aps[hf][:].rearrange("p t e -> p e t"))
             g = 2 * i + hf
             pending.append(lambda: V.quantize_mx(out=dc[g][:].bitcast(E5), scales=ds[g][:], in_=ai[:].rearrange("p e t -> p (e t)")))
 
+        vs = {}
+
         def back(i):
             y = zt[i]
-            ny[i] = one.tile([P, 6, D], F32, name="ny", tag="ny")
-
             dms = {}
+            vs[i] = one.tile([P, 4, D], F32, name="vs", tag="vs")
 
             def mul(n):
                 m = n % 4
-                dms[n] = ps.tile([P, D], F32, name="mm", tag="mm")
+                dms[n] = ps.tile([P, D], F32, name="mm", tag="hop", bufs=4)
                 T.matmul_mx(out=dms[n][:], lhsT=dct[i][n // 4][:, P * m:P * m + P].bitcast(E5), lhsT_scale=dst_[i][n // 4][:, P * m:P * m + P],
                             rhs=wc[:].bitcast(E4), rhs_scale=ws[:], start=True, stop=True)
 
             def add(n):
                 V.scalar_tensor_tensor(out=y[:, n, :], in0=dms[n][:], scalar=SQ8, in1=y[:, n, :], op0=OP.mult, op1=OP.add)
-                if n >= 2:
-                    G.tensor_scalar(ny[i][:, n - 2, :], y[:, n, :], -1.0, 0.0, OP.mult, OP.add)
 
-            return mul, add
+            def level(b1):
+                y4 = y[:].rearrange("p (m b) e -> p m b e", b=2)
+                m = slice(2 * b1, 2 * b1 + 2)
+                V.tensor_tensor(vs[i][:, m, :], y4[:, m, 0, :], y4[:, m, 1, :], OP.add)
+                V.tensor_tensor(y4[:, m, 1, :], y4[:, m, 0, :], y4[:, m, 1, :], OP.subtract)
+                k = 2 * b1 + 1
+                S.mul(y4[:, k - 1, 0, :], vs[i][:, k, :], -1.0)
+                S.mul(y4[:, k, 0, :], y4[:, k, 1, :], -1.0)
+
+            return mul, add, level
 
         def hops(i, dve=()):
             ts, tns, obs = {}, {}, {}
+            y4 = zt[i][:].rearrange("p (m b) e -> p m b e", b=2)
 
-            def first(db, b3):
-                if b3 == 0:
-                    ts[db] = two.tile([P, 2, 4, P], F32, name="t", tag="t")
-                    tns[db] = two.tile([P, 4, P], F32, name="tn", tag="tn")
-                hop = ps.tile([P, 4, P], F32, name="hop", tag="hop")
-                for o in range(4):
-                    j1, j0 = o // 2, o % 2
-                    for q in range(4):
-                        b1, b2 = q // 2, q % 2
-                        n = 4 * b1 + 2 * b2 + b3
-                        sl = slice(P * db, P * db + P)
-                        src = ny[i][:, n - 2, sl] if (b1 * j0 + b2 * j1) % 2 else zt[i][:, n, sl]
-                        T.matmul(hop[:, o, :], lhsT=src, rhs=ident_f[:], start=(q == 0), stop=(q == 3), is_transpose=True)
-                if (0, db, b3) in dve:
-                    V.tensor_copy(out=ts[db][:, b3, :, :], in_=hop[:])
+            def first(db, j2):
+                sl = slice(P * db, P * db + P)
+                t = two.tile([P, 2, 2, P], F32, name="t", tag="t", bufs=3)
+                tn = two.tile([P, 2, P], F32, name="tn", tag="tn", bufs=3)
+                hop = ps.tile([P, 2, 2, P], F32, name="hop", tag="hop", bufs=4)
+                for b1 in range(2):
+                    a = y4[:, 2 * b1, 1, sl] if j2 else vs[i][:, 2 * b1, sl]
+                    b = y4[:, 2 * b1 + 1, 1, sl] if j2 else vs[i][:, 2 * b1 + 1, sl]
+                    nb = y4[:, 2 * b1 + j2, 0, sl]
+                    for j1 in range(2):
+                        T.matmul(hop[:, b1, j1, :], lhsT=a, rhs=ident_f[:], start=True, stop=False, is_transpose=True)
+                        T.matmul(hop[:, b1, j1, :], lhsT=nb if j1 else b, rhs=ident_f[:], start=False, stop=True, is_transpose=True)
+                if (0, db, j2) in dve:
+                    V.tensor_copy(out=t[:], in_=hop[:])
                 else:
-                    S.copy(out=ts[db][:, b3, :, :], in_=hop[:])
-                if b3 == 1:
-                    S.mul(tns[db][:], hop[:], -1.0)
+                    S.copy(out=t[:], in_=hop[:])
+                S.mul(tn[:], hop[:, 1, :, :], -1.0)
+                ts[db, j2], tns[db, j2] = t, tn
 
             def second(db, j2):
                 if j2 == 0:
                     obs[db] = two.tile([P, P, NODES], F32, name="ob", tag="ob")
-                hop = ps.tile([P, 4, P], F32, name="hop", tag="hop")
-                for o in range(4):
-                    T.matmul(hop[:, o, :], lhsT=ts[db][:, 0, o, :], rhs=ident_f[:], start=True, stop=False, is_transpose=True)
-                    s = tns[db][:, o, :] if j2 else ts[db][:, 1, o, :]
-                    T.matmul(hop[:, o, :], lhsT=s, rhs=ident_f[:], start=False, stop=True, is_transpose=True)
+                t, tn = ts[db, j2], tns[db, j2]
+                hop = ps.tile([P, 2, 2, P], F32, name="hop", tag="hop", bufs=4)
+                for j1 in range(2):
+                    for j0 in range(2):
+                        T.matmul(hop[:, j1, j0, :], lhsT=t[:, 0, j1, :], rhs=ident_f[:], start=True, stop=False, is_transpose=True)
+                        T.matmul(hop[:, j1, j0, :], lhsT=tn[:, j1, :] if j0 else t[:, 1, j1, :], rhs=ident_f[:], start=False, stop=True, is_transpose=True)
+                o = obs[db][:, :, 4 * j2:4 * j2 + 4]
+                src = hop[:].rearrange("p a b d -> p d (a b)")
                 if (1, db, j2) in dve:
-                    V.tensor_scalar_mul(obs[db][:, :, 4 * j2:4 * j2 + 4], hop[:].rearrange("p o d -> p d o"), 0.125)
+                    V.tensor_scalar_mul(o, src, 0.125)
                 else:
-                    S.activation(out=obs[db][:, :, 4 * j2:4 * j2 + 4], in_=hop[:].rearrange("p o d -> p d o"), func=ACT.Copy, scale=0.125)
+                    S.activation(out=o, in_=src, func=ACT.Copy, scale=0.125)
                 if j2 == 1:
                     SY.dma_start(out=o2[P * i:P * i + P, 1024 * db:1024 * db + 1024], in_=obs[db][:].rearrange("p d j -> p (d j)"))
 
+            seq = [(db, j2) for db in range(4) for j2 in range(2)]
             out = []
-            for db in range(5):
-                for s in range(2):
-                    if db < 4:
-                        out.append(lambda db=db, s=s: first(db, s))
-                    if db > 0:
-                        out.append(lambda db=db, s=s: second(db - 1, s))
+            for k in range(10):
+                if k < 8:
+                    out.append(lambda k=k: first(*seq[k]))
+                if k >= 2:
+                    out.append(lambda k=k: second(*seq[k - 2]))
             return out
 
         accs = {}
@@ -395,106 +408,121 @@ def tile_waveletgatednet_v_kernel(tc, x, W, b, threshold, z, gated, grad_out, ou
             for p in ps:
                 p()
 
-        N_HOP_X = 5
-        N_HOP_P = 7
-        LAST = {(0, 3, 0), (0, 3, 1), (1, 2, 1), (1, 3, 0)}
+        CX, CP, CK = [1, 1, 1], [1, 1, 1, 2, 2, 2], [2, 1, 1, 0]
+        TX = [1, 1, 1, 1, 1, 1, 1, 1, 1]
+        LAST = {(0, 3, 0), (0, 3, 1), (1, 2, 0), (1, 3, 0)}
+        hop = []
 
-        with tc.manual_schedule():
+        def fill(n):
+            for j in range(min(n, len(hop))):
+                hop[0]()
+                hop.remove(hop[0])
+
+        if True:
             load_x(0)
-            load_x(1)
-            load_z(0)
-            load_h(0)
+            zt[0] = two.tile([P, NODES, D], F32, name="zt", tag="zt", bufs=3)
+            ht[0] = two.tile([P, NODES, D], F32, name="ht", tag="ht")
+            for hf in range(2):
+                n = slice(4 * hf, 4 * hf + 4)
+                SY.dma_start(out=zt[0][:, n, :], in_=z2[0:P, n, :])
+                SY.dma_start(out=ht[0][:, n, :], in_=h2[0:P, n, :])
             load_g(0)
             load_w()
+            load_x(1)
             load_z(1)
             load_h(1)
             run(do_x(0))
             gate_half(0, 0)
             gate_half(0, 1)
-            run(do_x(1))
-            early, bank, ahead = products(0)
-            early()
-            kq0 = kq(0)
-            run(kq0[:2])
+            parts = products(0)
+            kn = kq(0)
+            kn[0]()
+            kn[2]()
             flush()
-            run(kq0[2:])
+            kn[1]()
+            kn[3]()
+            parts[0]()
+            parts[3]()
             do_w()
-            load_x(2)
             gate_half(1, 0)
             gate_half(1, 1)
-            for bk in range(NB):
-                bank(bk)
-                ahead(bk)
-            hop = []
             for i in range(4):
+                for bk in range(NB):
+                    parts[1](bk)
+                    fill(CP[bk])
+                    parts[2](bk)
                 if i < 3:
                     load_g(i + 1)
                 move(i)
                 if i < 2:
                     load_z(i + 2)
                     load_h(i + 2)
+                    load_x(2 + i)
+                if i == 2:
+                    load_x(4)
+                if i == 3:
+                    load_x(5)
                 f = features(i)
                 qf = quant_features(i, f)
-                if i < 3:
-                    early, bank, ahead = products(i + 1)
-                    kn = kq(i + 1)
-                else:
-                    kn = do_x(5)
-                run(kn[:2])
-                run(hop[:len(hop) // 2])
+                for c, p in zip(CX, do_x(1 + i)):
+                    p()
+                    fill(c)
                 tokens(i, 0)
+                kn = [lambda: None] * 4
                 if i < 3:
-                    early()
-                run(hop[len(hop) // 2:])
+                    parts = products(i + 1)
+                    kn = kq(i + 1)
+                kn[0]()
+                fill(CK[0])
+                qf[0]()
+                mul, add, level = back(i)
+                for n in range(3):
+                    mul(n)
+                kn[1]()
+                fill(CK[1])
+                if i < 3:
+                    parts[0]()
+                fill(CK[2])
+                kn[2]()
+                fill(CK[3])
+                kn[3]()
+                qf[1]()
+                fill(99)
                 if i == 3:
                     weight_gradient(range(2))
-                qf[0]()
-                mul, add = back(i)
-                mul(0)
-                mul(1)
-                run(kn[2:])
-                qf[1]()
                 for n in range(NODES):
                     add(n)
-                    if n + 2 < NODES:
-                        mul(n + 2)
+                    if n + 3 < NODES:
+                        mul(n + 3)
+                    if n == 5 and i < 3:
+                        parts[3]()
+                    if n == 3:
+                        flush()
+                    if n % 4 == 3:
+                        level(n // 4)
                 if i < 2:
                     gate_half(i + 2, 0)
                     gate_half(i + 2, 1)
-                flush()
                 tokens(i, 1)
-                hop = hops(i, LAST if i == 3 else ())
-                if i < 3:
-                    weave(do_x(2 + i), hop[:N_HOP_X])
-                    load_x(3 + i)
-                    hop = hop[N_HOP_X:]
-                    for bk in range(NB):
-                        bank(bk)
-                        run(hop[N_HOP_P * bk // NB:N_HOP_P * (bk + 1) // NB])
-                        ahead(bk)
-                    hop = hop[N_HOP_P:]
-                    flush()
+                hop.extend(hops(i, LAST if i == 3 else ()))
             load_x(6)
             load_x(7)
-            weight_gradient(range(2, 6))
-            xa, xb = do_x(6), do_x(7)
-            xa[0]()
-            run(hop[:1])
-            xa[1]()
-            run(hop[1:3])
-            xa[2]()
-            run(hop[3:4])
-            xb[0]()
-            run(hop[4:6])
+            tail = do_x(5) + do_x(6) + do_x(7)
+            for j, p in enumerate(tail):
+                p()
+                fill(TX[j])
+                if j == 3:
+                    weight_gradient(range(2, 5))
+                if j in (1, 4, 7):
+                    pending[0]()
+                    pending.remove(pending[0])
+                if j == 4:
+                    weight_gradient([5])
+                if j == 7:
+                    weight_gradient([6])
+            fill(2)
             flush()
-            xb[1]()
-            run(hop[6:8])
-            xb[2]()
-            run(hop[8:9])
-            weight_gradient([6])
-            run(hop[9:11])
-            flush()
-            run(hop[11:13])
+            fill(1)
             weight_gradient([7])
             store_weight_gradient()
-            run(hop[13:])
+            fill(99)

@@ -102,12 +102,15 @@ def tile_waveletgatednet_v_kernel(tc, x, W, b, threshold, z, gated, grad_out, ou
         xr = {}
         pending = []
 
+        def load_x_half(g, hf):
+            t = two.tile([P, 2048], BF16, name="xr", tag="xr", bufs=2)
+            for h in range(2):
+                SY.dma_start(out=t[h::2, :], in_=x2[64 * g:64 * g + 64, 2048 * hf:2048 * hf + 2048])
+            return t[:, :]
+
         def load_x(g):
             for hf in range(2):
-                t = two.tile([P, 2048], BF16, name="xr", tag="xr", bufs=2)[:, :]
-                for h in range(2):
-                    SY.dma_start(out=t[h::2, :], in_=x2[64 * g:64 * g + 64, 2048 * hf:2048 * hf + 2048])
-                xr[g, hf] = t
+                xr[g, hf] = load_x_half(g, hf)
 
         def do_x(g):
             E = 256
@@ -299,12 +302,13 @@ def tile_waveletgatednet_v_kernel(tc, x, W, b, threshold, z, gated, grad_out, ou
             g = 2 * i + hf
             pending.append(lambda: V.quantize_mx(out=dc[g][:].bitcast(E5), scales=ds[g][:], in_=ai[:].rearrange("p e t -> p (e t)")))
 
-        vs = {}
+        terms = {}
 
         def back(i):
             y = zt[i]
+            y4 = y[:].rearrange("p (m b) e -> p m b e", b=2)
+            ny = one.tile([P, 6, D], F32, name="ny", tag="ny")
             dms = {}
-            vs[i] = one.tile([P, 4, D], F32, name="vs", tag="vs")
 
             def mul(n):
                 m = n % 4
@@ -314,21 +318,35 @@ def tile_waveletgatednet_v_kernel(tc, x, W, b, threshold, z, gated, grad_out, ou
 
             def add(n):
                 V.scalar_tensor_tensor(out=y[:, n, :], in0=dms[n][:], scalar=SQ8, in1=y[:, n, :], op0=OP.mult, op1=OP.add)
+                if i not in ON_VECTOR and n % 4:
+                    S.mul(ny[:, n - 1 - n // 4, :], y[:, n, :], -1.0)
+                if i in ON_VECTOR and n % 4 == 3:
+                    level(n // 4)
 
             def level(b1):
-                y4 = y[:].rearrange("p (m b) e -> p m b e", b=2)
                 m = slice(2 * b1, 2 * b1 + 2)
-                V.tensor_tensor(vs[i][:, m, :], y4[:, m, 0, :], y4[:, m, 1, :], OP.add)
-                V.tensor_tensor(y4[:, m, 1, :], y4[:, m, 0, :], y4[:, m, 1, :], OP.subtract)
                 k = 2 * b1 + 1
-                S.mul(y4[:, k - 1, 0, :], vs[i][:, k, :], -1.0)
+                V.tensor_tensor(ny[:, m, :], y4[:, m, 0, :], y4[:, m, 1, :], OP.add)
+                V.tensor_tensor(y4[:, m, 1, :], y4[:, m, 0, :], y4[:, m, 1, :], OP.subtract)
+                S.mul(y4[:, k - 1, 0, :], ny[:, k, :], -1.0)
                 S.mul(y4[:, k, 0, :], y4[:, k, 1, :], -1.0)
 
-            return mul, add, level
+            def two_terms(b1, j1, j2):
+                a = [y4[:, m, 1, :] if j2 else ny[:, m, :] for m in (2 * b1, 2 * b1 + 1)]
+                return [a[0], y4[:, 2 * b1 + j2, 0, :] if j1 else a[1]]
+
+            def four_terms(b1, j1, j2):
+                out = []
+                for q in range(4):
+                    n = 4 * b1 + q
+                    out.append(ny[:, n - 1 - b1, :] if (q // 2 * j1 + q % 2 * j2) % 2 else y[:, n, :])
+                return out
+
+            terms[i] = two_terms if i in ON_VECTOR else four_terms
+            return mul, add
 
         def hops(i, dve=()):
             ts, tns, obs = {}, {}, {}
-            y4 = zt[i][:].rearrange("p (m b) e -> p m b e", b=2)
 
             def first(db, j2):
                 sl = slice(P * db, P * db + P)
@@ -336,12 +354,10 @@ def tile_waveletgatednet_v_kernel(tc, x, W, b, threshold, z, gated, grad_out, ou
                 tn = two.tile([P, 2, P], F32, name="tn", tag="tn", bufs=3)
                 hop = ps.tile([P, 2, 2, P], F32, name="hop", tag="hop", bufs=4)
                 for b1 in range(2):
-                    a = y4[:, 2 * b1, 1, sl] if j2 else vs[i][:, 2 * b1, sl]
-                    b = y4[:, 2 * b1 + 1, 1, sl] if j2 else vs[i][:, 2 * b1 + 1, sl]
-                    nb = y4[:, 2 * b1 + j2, 0, sl]
                     for j1 in range(2):
-                        T.matmul(hop[:, b1, j1, :], lhsT=a, rhs=ident_f[:], start=True, stop=False, is_transpose=True)
-                        T.matmul(hop[:, b1, j1, :], lhsT=nb if j1 else b, rhs=ident_f[:], start=False, stop=True, is_transpose=True)
+                        parts = terms[i](b1, j1, j2)
+                        for k, a in enumerate(parts):
+                            T.matmul(hop[:, b1, j1, :], lhsT=a[:, sl], rhs=ident_f[:], start=(k == 0), stop=(k == len(parts) - 1), is_transpose=True)
                 if (0, db, j2) in dve:
                     V.tensor_copy(out=t[:], in_=hop[:])
                 else:
@@ -410,6 +426,7 @@ def tile_waveletgatednet_v_kernel(tc, x, W, b, threshold, z, gated, grad_out, ou
 
         CX, CP, CK = [1, 1, 1], [1, 1, 1, 2, 2, 2], [2, 1, 1, 0]
         TX = [1, 1, 1, 1, 1, 1, 1, 1, 1]
+        ON_VECTOR = {3}
         LAST = {(0, 3, 0), (0, 3, 1), (1, 2, 0), (1, 3, 0)}
         hop = []
 
@@ -419,20 +436,22 @@ def tile_waveletgatednet_v_kernel(tc, x, W, b, threshold, z, gated, grad_out, ou
                 hop.remove(hop[0])
 
         if True:
-            load_x(0)
+            xr[0, 0] = load_x_half(0, 0)
             zt[0] = two.tile([P, NODES, D], F32, name="zt", tag="zt", bufs=3)
             ht[0] = two.tile([P, NODES, D], F32, name="ht", tag="ht")
             for hf in range(2):
                 n = slice(4 * hf, 4 * hf + 4)
                 SY.dma_start(out=zt[0][:, n, :], in_=z2[0:P, n, :])
+                if hf == 0:
+                    xr[0, 1] = load_x_half(0, 1)
                 SY.dma_start(out=ht[0][:, n, :], in_=h2[0:P, n, :])
             load_g(0)
             load_w()
             load_x(1)
             load_z(1)
             load_h(1)
-            run(do_x(0))
             gate_half(0, 0)
+            run(do_x(0))
             gate_half(0, 1)
             parts = products(0)
             kn = kq(0)
@@ -475,7 +494,7 @@ def tile_waveletgatednet_v_kernel(tc, x, W, b, threshold, z, gated, grad_out, ou
                 kn[0]()
                 fill(CK[0])
                 qf[0]()
-                mul, add, level = back(i)
+                mul, add = back(i)
                 for n in range(3):
                     mul(n)
                 kn[1]()
@@ -498,8 +517,6 @@ def tile_waveletgatednet_v_kernel(tc, x, W, b, threshold, z, gated, grad_out, ou
                         parts[3]()
                     if n == 3:
                         flush()
-                    if n % 4 == 3:
-                        level(n // 4)
                 if i < 2:
                     gate_half(i + 2, 0)
                     gate_half(i + 2, 1)

@@ -26,9 +26,7 @@ ACT = mybir.ActivationFunctionType
 C = 1.0 / math.sqrt(8.0)
 SQ8 = math.sqrt(8.0)
 
-E_PE = 384
-E_DVE = D - E_PE
-NB = E_PE // 64
+BANKS = (7, 6, 6, 6)
 
 
 def tile_waveletgatednet_v_kernel(tc, x, W, b, threshold, z, gated, grad_out, out_0, out_1):
@@ -163,9 +161,8 @@ def tile_waveletgatednet_v_kernel(tc, x, W, b, threshold, z, gated, grad_out, ou
                 t[2] = lev.tile([P, 8 * E], F32, name="lB", tag="lB", bufs=2)
                 s = t[1][:].rearrange("p (b e f g) -> p b e f g", b=2, f=2, g=2)
                 o = t[2][:].rearrange("p (b f g e) -> p b f e g", b=2, f=2, g=2)
-                for b in range(2):
-                    for i, op in ((0, OP.add), (1, OP.subtract)):
-                        V.tensor_tensor(o[:, b, i, :, :], s[:, b, :, 0, :], s[:, b, :, 1, :], op)
+                for i, op in ((0, OP.add), (1, OP.subtract)):
+                    V.tensor_tensor(o[:, :, i, :, :], s[:, :, :, 0, :], s[:, :, :, 1, :], op)
 
             def l3():
                 t[3] = lev.tile([P, NODES, E], F32, name="lA", tag="lA", bufs=3)
@@ -211,6 +208,8 @@ def tile_waveletgatednet_v_kernel(tc, x, W, b, threshold, z, gated, grad_out, ou
 
         def products(i):
             k, q = zt[i], ht[i]
+            nb = BANKS[i]
+            e_pe = 64 * nb
 
             def pair(e0, w, dh):
                 sl = slice(e0, e0 + w)
@@ -232,7 +231,7 @@ def tile_waveletgatednet_v_kernel(tc, x, W, b, threshold, z, gated, grad_out, ou
                 for c in range(4):
                     T.matmul(dhs[bk][:, :, 16 * c:16 * c + 16], lhsT=gTs[bk][:, c, :], rhs=Hm[:], start=True, stop=True)
 
-            lv = wpt_parts(gt[i][:, 8 * E_PE:], E_DVE)
+            lv = wpt_parts(gt[i][:, 8 * e_pe:], D - e_pe)
 
             def early():
                 dz[i] = one.tile([P, NODES, D], BF16, name="dz", tag="dz")
@@ -249,12 +248,12 @@ def tile_waveletgatednet_v_kernel(tc, x, W, b, threshold, z, gated, grad_out, ou
                 if bk < 3:
                     lv[bk]()
                 if bk == 4:
-                    pair(E_PE, E_DVE, lv[3]()[:])
+                    pair(e_pe, D - e_pe, lv[3]()[:])
 
             def ahead(bk):
-                if bk + 2 < NB:
+                if bk + 2 < nb:
                     mm(bk + 2)
-                if bk + 3 < NB:
+                if bk + 3 < nb:
                     prep(bk + 3)
 
             return early, bank, ahead, start
@@ -424,10 +423,11 @@ def tile_waveletgatednet_v_kernel(tc, x, W, b, threshold, z, gated, grad_out, ou
             for p in ps:
                 p()
 
+        XS = [[],[1],[2],[3]]
         CX, CP, CK = [1, 1, 1], [1, 1, 1, 2, 2, 2], [2, 1, 1, 0]
         TX = [1, 1, 1, 1, 1, 1, 1, 1, 1]
         ON_VECTOR = {3}
-        LAST = {(0, 3, 0), (0, 3, 1), (1, 2, 0), (1, 3, 0)}
+        LAST = ()
         hop = []
 
         def fill(n):
@@ -447,7 +447,6 @@ def tile_waveletgatednet_v_kernel(tc, x, W, b, threshold, z, gated, grad_out, ou
                 SY.dma_start(out=ht[0][:, n, :], in_=h2[0:P, n, :])
             load_g(0)
             load_w()
-            load_x(1)
             load_z(1)
             load_h(1)
             gate_half(0, 0)
@@ -466,9 +465,9 @@ def tile_waveletgatednet_v_kernel(tc, x, W, b, threshold, z, gated, grad_out, ou
             gate_half(1, 0)
             gate_half(1, 1)
             for i in range(4):
-                for bk in range(NB):
+                for bk in range(BANKS[i]):
                     parts[1](bk)
-                    fill(CP[bk])
+                    fill(CP[min(bk, 5)])
                     parts[2](bk)
                 if i < 3:
                     load_g(i + 1)
@@ -476,16 +475,13 @@ def tile_waveletgatednet_v_kernel(tc, x, W, b, threshold, z, gated, grad_out, ou
                 if i < 2:
                     load_z(i + 2)
                     load_h(i + 2)
-                    load_x(2 + i)
-                if i == 2:
-                    load_x(4)
-                if i == 3:
-                    load_x(5)
                 f = features(i)
                 qf = quant_features(i, f)
-                for c, p in zip(CX, do_x(1 + i)):
-                    p()
-                    fill(c)
+                for g in XS[i]:
+                    load_x(g)
+                    for c, p in zip(CX, do_x(g)):
+                        p()
+                        fill(c)
                 tokens(i, 0)
                 kn = [lambda: None] * 4
                 if i < 3:
@@ -507,8 +503,6 @@ def tile_waveletgatednet_v_kernel(tc, x, W, b, threshold, z, gated, grad_out, ou
                 kn[3]()
                 qf[1]()
                 fill(99)
-                if i == 3:
-                    weight_gradient(range(2))
                 for n in range(NODES):
                     add(n)
                     if n + 3 < NODES:
@@ -522,21 +516,17 @@ def tile_waveletgatednet_v_kernel(tc, x, W, b, threshold, z, gated, grad_out, ou
                     gate_half(i + 2, 1)
                 tokens(i, 1)
                 hop.extend(hops(i, LAST if i == 3 else ()))
-            load_x(6)
-            load_x(7)
-            tail = do_x(5) + do_x(6) + do_x(7)
-            for j, p in enumerate(tail):
-                p()
-                fill(TX[j])
-                if j == 3:
-                    weight_gradient(range(2, 5))
-                if j in (1, 4, 7):
-                    pending[0]()
-                    pending.remove(pending[0])
-                if j == 4:
-                    weight_gradient([5])
-                if j == 7:
-                    weight_gradient([6])
+            for k, g in enumerate([4,5,6,7]):
+                load_x(g)
+                for p in do_x(g):
+                    p()
+                    fill(1)
+                if k > 0:
+                    while len(pending) > 1:
+                        pending[0]()
+                        pending.remove(pending[0])
+                    weight_gradient(range(4) if k == 1 else [])
+                    weight_gradient([g - 1])
             fill(2)
             flush()
             fill(1)

from contextlib import ExitStack
import math

import concourse.mybir as mybir
from concourse.masks import make_identity

ROWS = 512
L = 4096
NODES = 8
D = 512
P = 128

FLOPS = 2 * (2 * ROWS * NODES * D * D)
BYTES = 2 * ROWS * L * 2 + D * D * 2 + 2 * ROWS * L * 4 + ROWS * L * 4 + D * D * 4

F32 = mybir.dt.float32
BF16 = mybir.dt.bfloat16
I32 = mybir.dt.int32
U32 = mybir.dt.uint32
U8 = mybir.dt.uint8
E4 = mybir.dt.float8_e4m3fn_x4
E5 = mybir.dt.float8_e5m2_x4
OP = mybir.AluOpType
ACT = mybir.ActivationFunctionType

C = 1.0 / math.sqrt(8.0)
SQ8 = math.sqrt(8.0)

BANKS = (7, 6, 6, 6)


def tile_waveletgatednet_v_kernel(tc, x, W, b, threshold, z, gated, grad_out, out_0, out_1):
    nc = tc.nc
    V, S, T, G, SY = nc.vector, nc.scalar, nc.tensor, nc.gpsimd, nc.sync

    x2 = x.rearrange("b c l -> (b c) l")
    g2 = grad_out.rearrange("b c l -> (b c) l")
    o2 = out_0.rearrange("b c l -> (b c) l")
    z2 = z.rearrange("b c n e -> (b c) n e")
    h2 = gated.rearrange("b c n e -> (b c) n e")

    with ExitStack() as ctx:
        const = ctx.enter_context(tc.tile_pool(name="const", bufs=1))
        one = ctx.enter_context(tc.tile_pool(name="one", bufs=1))
        two = ctx.enter_context(tc.tile_pool(name="two", bufs=2))
        lev = ctx.enter_context(tc.tile_pool(name="lev", bufs=2))
        keep = ctx.enter_context(tc.tile_pool(name="keep", bufs=1))
        ps = ctx.enter_context(tc.psum_pool(name="ps", bufs=2))

        ident_f = const.tile([P, P], F32, name="ident_f")
        make_identity(nc, ident_f[:])
        ident_b = const.tile([P, P], BF16, name="ident_b")
        make_identity(nc, ident_b[:])
        pidx = const.tile([P, 1], I32, name="pidx")
        G.iota(pidx[:], [[0, 1]], base=0, channel_multiplier=1)
        podd = const.tile([P, 1], I32, name="podd")
        V.tensor_single_scalar(podd[:], pidx[:], 1, OP.bitwise_and)
        poddf = const.tile([P, 1], F32, name="poddf")
        V.tensor_copy(poddf[:], podd[:])
        sgn = const.tile([P, 1], F32, name="sgn")
        V.tensor_scalar(sgn[:], poddf[:], -2.0, 1.0, OP.mult, OP.add)

        def wpt(src, y1, y2, dst, E):
            s = src.rearrange("p (a two) -> p a two", two=2)
            for i, op in ((0, OP.add), (1, OP.subtract)):
                V.tensor_tensor(y1[:, i * 4 * E:(i + 1) * 4 * E], s[:, :, 0], s[:, :, 1], op)
            s = y1.rearrange("p (a two) -> p a two", two=2)
            o = y2.rearrange("p (b c f) -> p b c f", b=2, c=2)
            s4 = y1.rearrange("p (b a two) -> p b a two", b=2, two=2)
            for i, op in ((0, OP.add), (1, OP.subtract)):
                V.tensor_tensor(o[:, :, i, :], s4[:, :, :, 0], s4[:, :, :, 1], op)
            s4 = y2.rearrange("p (b a two) -> p b a two", b=4, two=2)
            o = dst.rearrange("p (b c) e -> p b c e", c=2)
            for i, op in ((0, OP.add), (1, OP.subtract)):
                V.tensor_tensor(o[:, :, i, :], s4[:, :, :, 0], s4[:, :, :, 1], op)

        Hm = const.tile([P, NODES, 16], BF16, name="Hm")
        h1 = const.tile([P, P], BF16, name="h1")
        hh2 = const.tile([P, P], BF16, name="hh2")
        wpt(ident_b[:], h1[:], hh2[:], Hm[:], 16)

        wc = const.tile([P, D], U32, name="wc", align_bytes=64)
        ws = const.tile([P, D], U8, name="ws", align_bytes=64)

        wr = {}

        def load_w():
            wr[0] = two.tile([P, 4, D], BF16, name="wraw", tag="ap")
            SY.dma_start(out=wr[0][:], in_=W.rearrange("(p j) d -> p j d", j=4))

        def do_w():
            wg = two.tile([P, D, 4], BF16, name="wg", tag="ai", align_bytes=64)
            S.copy(out=wg[:], in_=wr[0][:].rearrange("p j d -> p d j"))
            V.quantize_mx(out=wc[:].bitcast(E4), scales=ws[:], in_=wg[:].rearrange("p d j -> p (d j)"))

        xc = [keep.tile([P, D], U32, name="xc%d" % g, align_bytes=64) for g in range(8)]
        xs = [keep.tile([P, D], U8, name="xs%d" % g, align_bytes=64) for g in range(8)]
        dc = [keep.tile([P, D], U32, name="dc%d" % g, align_bytes=64) for g in range(8)]
        ds = [keep.tile([P, D], U8, name="ds%d" % g, align_bytes=64) for g in range(8)]
        xr = {}
        pending = []

        def load_x_half(g, hf):
            t = two.tile([P, 2048], BF16, name="xr", tag="xr", bufs=2)
            for h in range(2):
                SY.dma_start(out=t[h::2, :], in_=x2[64 * g:64 * g + 64, 2048 * hf:2048 * hf + 2048])
            return t[:, :]

        def load_x(g):
            for hf in range(2):
                xr[g, hf] = load_x_half(g, hf)

        def do_x(g):
            E = 256
            xi = two.tile([P, D, 4], BF16, name="xi", tag="xi", align_bytes=64)
            a1, a2 = [], []

            def l1():
                for hf in range(2):
                    t = xr[g, hf].rearrange("p (a two) -> p a two", two=2)
                    y1 = lev.tile([P, 1024], F32, name="lA", tag="lA", bufs=3)
                    V.scalar_tensor_tensor(out=y1[:], in0=t[:, :, 1], scalar=sgn[:], in1=t[:, :, 0], op0=OP.mult, op1=OP.add)
                    a1.append(y1)

            def l2():
                for hf in range(2):
                    y2 = lev.tile([P, 1024], F32, name="lB", tag="lB", bufs=2)
                    s = a1[hf][:].rearrange("p (e f g) -> p e f g", f=2, g=2)
                    o = y2[:].rearrange("p (f g e) -> p f e g", f=2, g=2)
                    for i, op in ((0, OP.add), (1, OP.subtract)):
                        V.tensor_tensor(o[:, i, :, :], s[:, :, 0, :], s[:, :, 1, :], op)
                    a2.append(y2)

            def l3():
                for hf in range(2):
                    y3 = lev.tile([P, 4, E], F32, name="lA", tag="lA", bufs=3)
                    s = a2[hf][:].rearrange("p (f g e) -> p f g e", f=2, g=2)
                    o = y3[:].rearrange("p (b c) e -> p b c e", c=2)
                    for i, op in ((0, OP.add), (1, OP.subtract)):
                        V.tensor_tensor(o[:, i, :, :], s[:, :, 0, :], s[:, :, 1, :], op)
                    S.activation(out=xi[:, E * hf:E * hf + E, :], in_=y3[:].rearrange("p t e -> p e t"), func=ACT.Copy, scale=C)
                pending.append(lambda: V.quantize_mx(out=xc[g][:].bitcast(E4), scales=xs[g][:], in_=xi[:].rearrange("p e t -> p (e t)")))

            return [l1, l2, l3]

        def flush():
            while pending:
                pending[0]()
                pending.remove(pending[0])

        def wpt_parts(src, E):
            t = {}

            def l1():
                t[1] = lev.tile([P, 8 * E], F32, name="lA", tag="lA", bufs=3)
                s = src.rearrange("p (a two) -> p a two", two=2)
                for i, op in ((0, OP.add), (1, OP.subtract)):
                    V.tensor_tensor(t[1][:, i * 4 * E:(i + 1) * 4 * E], s[:, :, 0], s[:, :, 1], op)

            def l2():
                t[2] = lev.tile([P, 8 * E], F32, name="lB", tag="lB", bufs=2)
                s = t[1][:].rearrange("p (b e f g) -> p b e f g", b=2, f=2, g=2)
                o = t[2][:].rearrange("p (b f g e) -> p b f e g", b=2, f=2, g=2)
                for i, op in ((0, OP.add), (1, OP.subtract)):
                    V.tensor_tensor(o[:, :, i, :, :], s[:, :, :, 0, :], s[:, :, :, 1, :], op)

            def l3():
                t[3] = lev.tile([P, NODES, E], F32, name="lA", tag="lA", bufs=3)
                o = t[3][:].rearrange("p (b c f) e -> p c b f e", b=2, c=2)
                s2 = t[2][:].rearrange("p (b f g e) -> p g b f e", b=2, f=2, g=2)
                for i, op in ((0, OP.add), (1, OP.subtract)):
                    V.tensor_tensor(o[:, i, :, :, :], s2[:, 0, :, :, :], s2[:, 1, :, :, :], op)

            return [l1, l2, l3, lambda: t[3]]

        zt, ht, gt, dz, dct, dst_, ny = {}, {}, {}, {}, {}, {}, {}

        def load_z(i):
            zt[i] = two.tile([P, NODES, D], F32, name="zt", tag="zt", bufs=3)
            for hf in range(2):
                n = slice(4 * hf, 4 * hf + 4)
                SY.dma_start(out=zt[i][:, n, :], in_=z2[P * i:P * i + P, n, :])

        def load_h(i):
            ht[i] = two.tile([P, NODES, D], F32, name="ht", tag="ht")
            for hf in range(2):
                n = slice(4 * hf, 4 * hf + 4)
                SY.dma_start(out=ht[i][:, n, :], in_=h2[P * i:P * i + P, n, :])

        def load_g(i):
            gt[i] = one.tile([P, L], BF16, name="gt", tag="gt")
            SY.dma_start(out=gt[i][:], in_=g2[P * i:P * i + P, :])

        def kq(i):
            def k(hf):
                n = slice(4 * hf, 4 * hf + 4)
                V.scalar_tensor_tensor(out=zt[i][:, n, :], in0=ht[i][:, n, :], scalar=0.0, in1=zt[i][:, n, :], op0=OP.not_equal, op1=OP.mult)

            def q(hf):
                n = slice(4 * hf, 4 * hf + 4)
                V.scalar_tensor_tensor(out=ht[i][:, n, :], in0=zt[i][:, n, :], scalar=1.0, in1=ht[i][:, n, :], op0=OP.subtract, op1=OP.mult)

            return [lambda: k(0), lambda: k(1), lambda: q(0), lambda: q(1)]

        def gate_half(i, hf):
            n = slice(4 * hf, 4 * hf + 4)
            S.activation(out=zt[i][:, n, :], in_=zt[i][:, n, :], func=ACT.Sigmoid)

        def products(i):
            k, q = zt[i], ht[i]
            nb = BANKS[i]
            e_pe = 64 * nb

            def pair(e0, w, dh):
                sl = slice(e0, e0 + w)
                V.scalar_tensor_tensor(out=dz[i][:, :, sl], in0=dh, scalar=-C, in1=q[:, :, sl], op0=OP.mult, op1=OP.mult)
                V.scalar_tensor_tensor(out=k[:, :, sl], in0=k[:, :, sl], scalar=1.0, in1=dh, op0=OP.add, op1=OP.mult)

            gTs, dhs = {}, {}

            def prep(bk):
                tp = ps.tile([P, 4, P], BF16, name="tp", tag="tp")
                for c in range(4):
                    p0 = (4 * bk + c) * P
                    T.transpose(tp[:, c, :], gt[i][:, p0:p0 + P], ident_b[:])
                gTs[bk] = two.tile([P, 4, P], BF16, name="gT", tag="gT", bufs=4)
                S.copy(out=gTs[bk][:], in_=tp[:])

            def mm(bk):
                dhs[bk] = ps.tile([P, NODES, 64], F32, name="dh", tag="dh")
                for c in range(4):
                    T.matmul(dhs[bk][:, :, 16 * c:16 * c + 16], lhsT=gTs[bk][:, c, :], rhs=Hm[:], start=True, stop=True)

            lv = wpt_parts(gt[i][:, 8 * e_pe:], D - e_pe)

            def early():
                dz[i] = one.tile([P, NODES, D], BF16, name="dz", tag="dz")
                prep(0)
                prep(1)
                prep(2)

            def start():
                mm(0)
                mm(1)

            def bank(bk):
                pair(64 * bk, 64, dhs[bk][:])
                if bk < 3:
                    lv[bk]()
                if bk == 4:
                    pair(e_pe, D - e_pe, lv[3]()[:])

            def ahead(bk):
                if bk + 2 < nb:
                    mm(bk + 2)
                if bk + 3 < nb:
                    prep(bk + 3)

            return early, bank, ahead, start

        def features(i):
            w = dz[i][:].rearrange("p n e -> p (n e)").bitcast(F32)
            tis = []
            for hf in range(2):
                ti = two.tile([P, 4, P, 4], BF16, name="ti", tag="ti", align_bytes=64)
                for pr in range(2):
                    rt = ps.tile([P, 2, 2, P], F32, name="tp", tag="tp")
                    for m in range(2):
                        n = 4 * hf + 2 * pr + m
                        for u in range(2):
                            T.transpose(rt[:, m, u, :], w[:, 256 * n + u:256 * n + 256:2], ident_f[:])
                    o = ti[:, 2 * pr:2 * pr + 2, :, :].rearrange("p m r t -> p (m r t)").bitcast(F32)
                    S.copy(out=o.rearrange("p (m r u) -> p m r u", m=2, u=2), in_=rt[:].rearrange("p m u r -> p m r u"))
                tis.append(ti)

            return tis

        def quant_features(i, tis):
            dct[i], dst_[i] = [], []

            def half(ti):
                c = two.tile([P, D], U32, name="dct", tag="dct", bufs=2, align_bytes=64)
                s = two.tile([P, D], U8, name="dst", tag="dst", bufs=2, align_bytes=64)
                V.quantize_mx(out=c[:].bitcast(E5), scales=s[:], in_=ti[:].rearrange("p n r t -> p (n r t)"))
                dct[i].append(c)
                dst_[i].append(s)

            return [lambda ti=ti: half(ti) for ti in tis]

        aps = {}

        def move(i):
            for hf in range(2):
                aps[hf] = two.tile([P, 4, D], BF16, name="ap", tag="ap")
                for h in range(2):
                    SY.dma_start(out=aps[hf][h::2, :, :], in_=dz[i][64 * hf:64 * hf + 64, 4 * h:4 * h + 4, :])

        def tokens(i, hf):
            ai = two.tile([P, D, 4], BF16, name="ai", tag="ai", align_bytes=64)
            S.copy(out=ai[:], in_=aps[hf][:].rearrange("p t e -> p e t"))
            g = 2 * i + hf
            pending.append(lambda: V.quantize_mx(out=dc[g][:].bitcast(E5), scales=ds[g][:], in_=ai[:].rearrange("p e t -> p (e t)")))

        terms = {}

        def back(i):
            y = zt[i]
            y4 = y[:].rearrange("p (m b) e -> p m b e", b=2)
            ny = one.tile([P, 6, D], F32, name="ny", tag="ny")
            dms = {}

            def mul(n):
                m = n % 4
                dms[n] = ps.tile([P, D], F32, name="mm", tag="hop", bufs=4)
                T.matmul_mx(out=dms[n][:], lhsT=dct[i][n // 4][:, P * m:P * m + P].bitcast(E5), lhsT_scale=dst_[i][n // 4][:, P * m:P * m + P],
                            rhs=wc[:].bitcast(E4), rhs_scale=ws[:], start=True, stop=True)

            def add(n):
                V.scalar_tensor_tensor(out=y[:, n, :], in0=dms[n][:], scalar=SQ8, in1=y[:, n, :], op0=OP.mult, op1=OP.add)
                if i not in ON_VECTOR and n % 4:
                    S.mul(ny[:, n - 1 - n // 4, :], y[:, n, :], -1.0)
                if i in ON_VECTOR and n % 4 == 3:
                    level(n // 4)

            def level(b1):
                m = slice(2 * b1, 2 * b1 + 2)
                k = 2 * b1 + 1
                V.tensor_tensor(ny[:, m, :], y4[:, m, 0, :], y4[:, m, 1, :], OP.add)
                V.tensor_tensor(y4[:, m, 1, :], y4[:, m, 0, :], y4[:, m, 1, :], OP.subtract)
                S.mul(y4[:, k - 1, 0, :], ny[:, k, :], -1.0)
                S.mul(y4[:, k, 0, :], y4[:, k, 1, :], -1.0)

            def two_terms(b1, j1, j2):
                a = [y4[:, m, 1, :] if j2 else ny[:, m, :] for m in (2 * b1, 2 * b1 + 1)]
                return [a[0], y4[:, 2 * b1 + j2, 0, :] if j1 else a[1]]

            def four_terms(b1, j1, j2):
                out = []
                for q in range(4):
                    n = 4 * b1 + q
                    out.append(ny[:, n - 1 - b1, :] if (q // 2 * j1 + q % 2 * j2) % 2 else y[:, n, :])
                return out

            terms[i] = two_terms if i in ON_VECTOR else four_terms
            return mul, add

        def hops(i, dve=()):
            ts, tns, obs = {}, {}, {}

            def first(db, j2):
                sl = slice(P * db, P * db + P)
                t = two.tile([P, 2, 2, P], F32, name="t", tag="t", bufs=3)
                tn = two.tile([P, 2, P], F32, name="tn", tag="tn", bufs=3)
                hop = ps.tile([P, 2, 2, P], F32, name="hop", tag="hop", bufs=4)
                for b1 in range(2):
                    for j1 in range(2):
                        parts = terms[i](b1, j1, j2)
                        for k, a in enumerate(parts):
                            T.matmul(hop[:, b1, j1, :], lhsT=a[:, sl], rhs=ident_f[:], start=(k == 0), stop=(k == len(parts) - 1), is_transpose=True)
                if (0, db, j2) in dve:
                    V.tensor_copy(out=t[:], in_=hop[:])
                else:
                    S.copy(out=t[:], in_=hop[:])
                S.mul(tn[:], hop[:, 1, :, :], -1.0)
                ts[db, j2], tns[db, j2] = t, tn

            def second(db, j2):
                if j2 == 0:
                    obs[db] = two.tile([P, P, NODES], F32, name="ob", tag="ob")
                t, tn = ts[db, j2], tns[db, j2]
                hop = ps.tile([P, 2, 2, P], F32, name="hop", tag="hop", bufs=4)
                for j1 in range(2):
                    for j0 in range(2):
                        T.matmul(hop[:, j1, j0, :], lhsT=t[:, 0, j1, :], rhs=ident_f[:], start=True, stop=False, is_transpose=True)
                        T.matmul(hop[:, j1, j0, :], lhsT=tn[:, j1, :] if j0 else t[:, 1, j1, :], rhs=ident_f[:], start=False, stop=True, is_transpose=True)
                o = obs[db][:, :, 4 * j2:4 * j2 + 4]
                src = hop[:].rearrange("p a b d -> p d (a b)")
                if (1, db, j2) in dve:
                    V.tensor_scalar_mul(o, src, 0.125)
                else:
                    S.activation(out=o, in_=src, func=ACT.Copy, scale=0.125)
                if j2 == 1:
                    SY.dma_start(out=o2[P * i:P * i + P, 1024 * db:1024 * db + 1024], in_=obs[db][:].rearrange("p d j -> p (d j)"))

            seq = [(db, j2) for db in range(4) for j2 in range(2)]
            out = []
            for k in range(10):
                if k < 8:
                    out.append(lambda k=k: first(*seq[k]))
                if k >= 2:
                    out.append(lambda k=k: second(*seq[k - 2]))
            return out

        accs = {}

        def weight_gradient(gs):
            for g in gs:
                for mt in range(4):
                    if g == 0:
                        accs[mt] = ps.tile([P, D], F32, name="acc", tag="dh" if mt < 2 else "tp")
                    msl = slice(P * mt, P * mt + P)
                    T.matmul_mx(out=accs[mt][:], lhsT=dc[g][:, msl].bitcast(E5), lhsT_scale=ds[g][:, msl],
                                rhs=xc[g][:].bitcast(E4), rhs_scale=xs[g][:], start=(g == 0), stop=(g == 7))

        def store_weight_gradient():
            for mt in range(4):
                r1 = lev.tile([P, D], F32, name="r1", tag="lA" if mt < 2 else "lB", bufs=3 if mt < 2 else 2)
                if mt % 2:
                    S.copy(out=r1[:], in_=accs[mt][:])
                else:
                    V.tensor_copy(out=r1[:], in_=accs[mt][:])
                SY.dma_start(out=out_1[P * mt:P * mt + P, :], in_=r1[:])

        def weave(first, second):
            n = max(len(first), 1)
            for j in range(n):
                if j < len(first):
                    first[j]()
                for s in second[len(second) * j // n:len(second) * (j + 1) // n]:
                    s()

        def run(ps):
            for p in ps:
                p()

        XS = [[],[1],[2],[3]]
        CX, CP, CK = [1, 1, 1], [1, 1, 1, 2, 2, 2], [2, 1, 1, 0]
        TX = [1, 1, 1, 1, 1, 1, 1, 1, 1]
        ON_VECTOR = {3}
        LAST = ()
        hop = []

        def fill(n):
            for j in range(min(n, len(hop))):
                hop[0]()
                hop.remove(hop[0])

        if True:
            xr[0, 0] = load_x_half(0, 0)
            zt[0] = two.tile([P, NODES, D], F32, name="zt", tag="zt", bufs=3)
            ht[0] = two.tile([P, NODES, D], F32, name="ht", tag="ht")
            for hf in range(2):
                n = slice(4 * hf, 4 * hf + 4)
                SY.dma_start(out=zt[0][:, n, :], in_=z2[0:P, n, :])
                if hf == 0:
                    xr[0, 1] = load_x_half(0, 1)
                SY.dma_start(out=ht[0][:, n, :], in_=h2[0:P, n, :])
            load_g(0)
            load_w()
            load_z(1)
            load_h(1)
            gate_half(0, 0)
            run(do_x(0))
            gate_half(0, 1)
            parts = products(0)
            kn = kq(0)
            kn[0]()
            kn[2]()
            flush()
            kn[1]()
            kn[3]()
            parts[0]()
            parts[3]()
            do_w()
            gate_half(1, 0)
            gate_half(1, 1)
            for i in range(4):
                for bk in range(BANKS[i]):
                    parts[1](bk)
                    fill(CP[min(bk, 5)])
                    parts[2](bk)
                if i < 3:
                    load_g(i + 1)
                move(i)
                if i < 2:
                    load_z(i + 2)
                    load_h(i + 2)
                f = features(i)
                qf = quant_features(i, f)
                for g in XS[i]:
                    load_x(g)
                    for c, p in zip(CX, do_x(g)):
                        p()
                        fill(c)
                tokens(i, 0)
                kn = [lambda: None] * 4
                if i < 3:
                    parts = products(i + 1)
                    kn = kq(i + 1)
                kn[0]()
                fill(CK[0])
                qf[0]()
                mul, add = back(i)
                for n in range(3):
                    mul(n)
                kn[1]()
                fill(CK[1])
                if i < 3:
                    parts[0]()
                fill(CK[2])
                kn[2]()
                fill(CK[3])
                kn[3]()
                qf[1]()
                fill(99)
                for n in range(NODES):
                    add(n)
                    if n + 3 < NODES:
                        mul(n + 3)
                    if n == 5 and i < 3:
                        parts[3]()
                    if n == 3:
                        flush()
                if i < 2:
                    gate_half(i + 2, 0)
                    gate_half(i + 2, 1)
                tokens(i, 1)
                hop.extend(hops(i, LAST if i == 3 else ()))
            for k, g in enumerate([4,5,6,7]):
                load_x(g)
                for p in do_x(g):
                    p()
                    fill(1)
                if k > 0:
                    while len(pending) > 1:
                        pending[0]()
                        pending.remove(pending[0])
                    weight_gradient(range(4) if k == 1 else [])
                    weight_gradient([g - 1])
            fill(2)
            flush()
            fill(1)
            weight_gradient([7])
            store_weight_gradient()
            fill(99)
